import numpy as np
import ml_dtypes


def mxq(x, axis, fmt="e4m3"):
    dtype, down = {"e4m3": (ml_dtypes.float8_e4m3fn, 7), "e5m2": (ml_dtypes.float8_e5m2, 14)}[fmt]
    v = np.moveaxis(np.asarray(x, np.float32).astype(ml_dtypes.bfloat16).astype(np.float64), axis, -1)
    blocks = v.reshape(v.shape[:-1] + (-1, 32))
    amax = np.abs(blocks).max(-1, keepdims=True)
    byte = np.maximum(np.where(amax > 0, np.frexp(amax)[1] - 1 + 127, 0) - down, 1)
    scale = np.exp2(byte - 127.0)
    codes = (blocks / scale).astype(np.float32).astype(dtype).astype(np.float64)
    return np.moveaxis((codes * scale).reshape(v.shape), -1, axis)


WIDE = False


def mx_kscale(k):
    if not WIDE:
        return np.ones(k)
    levels = np.array([30, -30])
    if k % 512:
        return np.exp2(np.random.permutation(np.resize(levels, k // 32))).repeat(32)
    a = np.empty((k // 512, 16))
    for p in range(k // 512):
        a[p, :8] = np.random.permutation(np.resize(levels, 8))
        for g in range(8):
            far = levels[np.abs(levels - a[p, g]) >= 10]
            a[p, g + 8] = far[np.random.randint(len(far))]
    return np.exp2(a.ravel()).repeat(32)


BF16 = ml_dtypes.bfloat16


def bf(x):
    return np.asarray(x, np.float32).astype(BF16)


def f64(x):
    return np.asarray(x).astype(np.float64)


B, C, D, T, H, W, P = 1, 1024, 512, 8, 16, 16, 2
N = T * H * W
BN_EPS = 1e-5


def setup_inputs():
    s = mx_kscale(D)
    return {"y": bf(np.random.standard_normal((B, D, T, H, W)) * 0.3 * np.sqrt(D) * s[None, :, None, None, None]),
            "w_w": bf(np.random.standard_normal((C, D)) / (0.3 * D) / s[None, :]),
            "w_b": bf(np.random.standard_normal(C) * 0.3),
            "bn_gamma": bf(np.random.standard_normal(C))}


def reference(y, w_w, w_b, bn_gamma):
    wy = (mxq(f64(w_w), 1, "e5m2") @ mxq(f64(y).reshape(B, D, N), 1, "e5m2")) + f64(w_b)[None, :, None]
    wy = wy.reshape(B, C, T, H, W)
    mean = wy.mean(axis=(0, 2, 3, 4))
    var = wy.var(axis=(0, 2, 3, 4))
    return wy, mean, f64(bn_gamma) / np.sqrt(var + BN_EPS)

@@ -1,0 +1,211 @@
+from contextlib import ExitStack
+
+import concourse.mybir as mybir
+from concourse.masks import make_identity
+
+FLOPS = 2 * 1024 * 512 * 2048
+
+F32 = mybir.dt.float32
+BF16 = mybir.dt.bfloat16
+U32 = mybir.dt.uint32
+U8 = mybir.dt.uint8
+FP8X4 = mybir.dt.float8_e5m2_x4
+ACT = mybir.ActivationFunctionType
+ALU = mybir.AluOpType
+
+P = 128
+C_OUT = 1024
+K = 512
+N = 2048
+PACK = 4
+M_TILES = C_OUT // P
+N_TILE = 512
+CHUNKS = N // N_TILE
+BN_EPS = 1e-5
+
+Y0_PIECES = (("v", 0, 256), ("v", 256, 384), ("s", 384, 512))
+Y1_PIECES = (("v", 0, 288), ("s", 288, 512))
+SKEW = 3
+
+
+def bank_order():
+    order = [(0, 0), (1, 0), (0, 1), (1, 1)]
+    for m in range(2, M_TILES):
+        order.extend([(m, 0), (m, 1)])
+    for m in range(SKEW):
+        order.append((m, 2))
+    for m in range(SKEW):
+        order.append((m, 3))
+    for m in range(SKEW, M_TILES):
+        order.extend([(m, 2), (m, 3)])
+    return order
+
+
+def tile_nonlocalblocknd_pc_kernel(tc, y, w_w, w_b, bn_gamma, out_0, out_1, out_2):
+    nc = tc.nc
+    y_v = y.rearrange("b d t h w -> (b d) (t h w)").rearrange("(p j) n -> p j n", j=PACK)
+    w_v = w_w.rearrange("(p m) k -> p m k", m=M_TILES)
+    o_v = out_0.rearrange("b c t h w -> (b c) (t h w)").rearrange("(p m) n -> p m n", m=M_TILES)
+
+    with ExitStack() as ctx:
+        ctx.enter_context(tc.manual_schedule())
+        keep = ctx.enter_context(tc.tile_pool(name="keep", bufs=1))
+        psum = ctx.enter_context(tc.psum_pool(name="psum", bufs=8))
+
+        b_sb = keep.tile([P, M_TILES], BF16, name="b_sb")
+        g_sb = keep.tile([P, M_TILES], BF16, name="g_sb")
+        nc.scalar.dma_start(out=b_sb[:], in_=w_b.rearrange("(p m) -> p m", m=M_TILES))
+        nc.scalar.dma_start(out=g_sb[:], in_=bn_gamma.rearrange("(p m) -> p m", m=M_TILES))
+
+        one = keep.tile([P, 1], F32, name="one")
+        junk = keep.tile([P, 1], F32, name="junk")
+        nc.vector.memset(one[:], 1.0)
+        nc.scalar.activation(out=junk[:], in_=one[:], func=ACT.Sqrt)
+
+        ident = keep.tile([P, P], F32, name="ident")
+        make_identity(nc, ident[:])
+
+        w_raw = keep.tile([P, M_TILES, K], BF16, name="w_raw")
+        y_raw = []
+        for j in range(CHUNKS):
+            y_raw.append(keep.tile([P, PACK, N_TILE], BF16, name="y_raw%d" % j))
+        nc.sync.dma_start(out=w_raw[:, 0:2, :], in_=w_v[:, 0:2, :])
+        nc.sync.dma_start(out=y_raw[0][:, :, 0:256], in_=y_v[:, :, 0:256])
+        nc.sync.dma_start(out=y_raw[0][:, :, 256:512], in_=y_v[:, :, 256:512])
+        nc.sync.dma_start(out=y_raw[1][:], in_=y_v[:, :, N_TILE:2 * N_TILE])
+        nc.sync.dma_start(out=w_raw[:, 2:M_TILES, :], in_=w_v[:, 2:M_TILES, :])
+        nc.sync.dma_start(out=y_raw[2][:], in_=y_v[:, :, 2 * N_TILE:3 * N_TILE])
+        nc.sync.dma_start(out=y_raw[3][:], in_=y_v[:, :, 3 * N_TILE:4 * N_TILE])
+
+        y_grp = {}
+        y_codes = {}
+        y_scales = {}
+        w_codes = keep.tile([P, M_TILES * P], U32, name="w_codes", align_bytes=64)
+        w_scales = keep.tile([P, M_TILES * P], U8, name="w_scales", align_bytes=64)
+        w_words = w_raw[:].rearrange("p m k -> p (m k)").bitcast(F32)
+
+        def interleave_y(j, pieces):
+            grp = keep.tile([P, N_TILE, PACK], BF16, name="y_grp%d" % j, align_bytes=64)
+            y_grp[j] = grp
+            for eng, c0, c1 in pieces:
+                src = y_raw[j][:, :, c0:c1].rearrange("p t c -> p c t")
+                if eng == "v":
+                    nc.vector.tensor_copy(out=grp[:, c0:c1, :], in_=src)
+                else:
+                    nc.scalar.copy(out=grp[:, c0:c1, :], in_=src)
+
+        def interleave_y_gpsimd(j):
+            grp = keep.tile([P, N_TILE, PACK], BF16, name="y_grp%d" % j, tag="shared_grp", align_bytes=64)
+            y_grp[j] = grp
+            nc.gpsimd.tensor_scalar(
+                out=grp[:],
+                in0=y_raw[j][:].rearrange("p t c -> p c t"),
+                scalar1=1.0,
+                scalar2=0.0,
+                op0=ALU.mult,
+                op1=ALU.add,
+            )
+
+        def quantize_y(j):
+            codes = keep.tile([P, N_TILE], U32, name="y_codes%d" % j, align_bytes=64)
+            scales = keep.tile([P, N_TILE], U8, name="y_scales%d" % j, align_bytes=64)
+            y_codes[j] = codes
+            y_scales[j] = scales
+            nc.vector.quantize_mx(
+                out=codes[:].bitcast(FP8X4),
+                scales=scales[:],
+                in_=y_grp[j][:].rearrange("p c t -> p (c t)"),
+            )
+
+        def transpose_w(q, grp_half):
+            wt = psum.tile([P, 2, 2, P], F32, name="wt", tag="bank")
+            for mm in range(2):
+                for u in range(2):
+                    base = 256 * (2 * q + mm)
+                    nc.tensor.transpose(wt[:, mm, u, :], w_words[:, base + u:base + 256:2], ident[:])
+            nc.scalar.copy(out=grp_half, in_=wt[:].rearrange("p m u r -> p m r u"))
+
+        def quantize_w(q0, pairs, grp):
+            cols = slice(2 * P * q0, 2 * P * (q0 + pairs))
+            nc.vector.quantize_mx(
+                out=w_codes[:, cols].bitcast(FP8X4),
+                scales=w_scales[:, cols],
+                in_=grp[:].rearrange("p m r u -> p (m r u)").bitcast(BF16),
+            )
+
+        stats = keep.tile([P, M_TILES, CHUNKS, 6], F32, name="stats")
+        mv = keep.tile([P, M_TILES, 2], F32, name="mv")
+        res = {}
+        seen = {}
+
+        def bank(m, j):
+            h = j // 2
+            e = j % 2
+            if (m, h) not in res:
+                res[(m, h)] = keep.tile([P, 2 * N_TILE], F32, name="res%d_%d" % (m, h))
+            r = res[(m, h)]
+            cols = slice(P * m, P * (m + 1))
+            acc = psum.tile([P, N_TILE], F32, name="acc", tag="bank")
+            nc.tensor.matmul_mx(
+                out=acc[:],
+                lhsT=w_codes[:, cols].bitcast(FP8X4),
+                lhsT_scale=w_scales[:, cols],
+                rhs=y_codes[j][:].bitcast(FP8X4),
+                rhs_scale=y_scales[j][:],
+                start=True,
+                stop=True,
+            )
+            nc.scalar.activation(
+                out=r[:, e * N_TILE:(e + 1) * N_TILE],
+                in_=acc[:],
+                func=ACT.Identity,
+                bias=b_sb[:, m:m + 1],
+                scale=1.0,
+            )
+            nc.vector.bn_stats(out=stats[:, m, j, :], in_=acc[:])
+            seen[(m, h)] = seen.get((m, h), 0) + 1
+            seen[m] = seen.get(m, 0) + 1
+            if (m, h) == (M_TILES - 1, 1):
+                nc.sync.dma_start(out=o_v[:, m, j * N_TILE:(j + 1) * N_TILE], in_=r[:, e * N_TILE:(e + 1) * N_TILE])
+            elif seen[(m, h)] == 2:
+                nc.sync.dma_start(out=o_v[:, m, 2 * h * N_TILE:2 * (h + 1) * N_TILE], in_=r[:])
+            if seen[m] == CHUNKS:
+                nc.vector.bn_aggr(out=mv[:, m, :], in_=stats[:, m, :, :].rearrange("p j s -> p (j s)"))
+
+        w_grp0 = keep.tile([P, 2, P, 2], F32, name="w_grp0", align_bytes=64)
+        w_grp1 = keep.tile([P, 2, P, 2], F32, name="w_grp1", align_bytes=64)
+        transpose_w(0, w_grp0[:])
+        interleave_y(0, Y0_PIECES)
+        quantize_w(0, 1, w_grp0)
+        quantize_y(0)
+        interleave_y(1, Y1_PIECES)
+        quantize_y(1)
+
+        order = bank_order()
+        for i in range(len(order)):
+            if i == 2:
+                transpose_w(1, w_grp1[:])
+                w_grp23 = keep.tile([P, 4, P, 2], F32, name="w_grp23", tag="shared_grp", align_bytes=64)
+                transpose_w(2, w_grp23[:, 0:2, :, :])
+            if i == 3:
+                transpose_w(3, w_grp23[:, 2:4, :, :])
+                quantize_w(1, 1, w_grp1)
+                quantize_w(2, 2, w_grp23)
+                interleave_y_gpsimd(2)
+            if i == 10:
+                quantize_y(2)
+                interleave_y_gpsimd(3)
+            if i == 16:
+                quantize_y(3)
+            bank(order[i][0], order[i][1])
+
+        sd = keep.tile([P, M_TILES], F32, name="sd")
+        rs = keep.tile([P, M_TILES], F32, name="rs")
+        gain = keep.tile([P, M_TILES], F32, name="gain")
+        mean = keep.tile([P, M_TILES], F32, name="mean")
+        nc.scalar.activation(out=sd[:], in_=mv[:, :, 1], func=ACT.Sqrt, bias=BN_EPS, scale=1.0)
+        nc.vector.reciprocal(out=rs[:], in_=sd[:])
+        nc.vector.tensor_mul(out=gain[:], in0=rs[:], in1=g_sb[:])
+        nc.sync.dma_start(out=out_2.rearrange("(p m) -> p m", m=M_TILES), in_=gain[:])
+        nc.vector.tensor_add(out=mean[:], in0=mv[:, :, 0], in1=b_sb[:])
+        nc.scalar.dma_start(out=out_1.rearrange("(p m) -> p m", m=M_TILES), in_=mean[:])

@@ -25,6 +25,7 @@ BN_EPS = 1e-5
 
 Y0_PIECES = (("v", 0, 256), ("v", 256, 384), ("s", 384, 512))
 Y1_PIECES = (("v", 0, 288), ("s", 288, 512))
+Y23_PIECES = (("v", 0, 320), ("s", 320, 512))
 SKEW = 3
 
 
@@ -191,10 +192,10 @@ def tile_nonlocalblocknd_pc_kernel(tc, y, w_w, w_b, bn_gamma, out_0, out_1, out_
                 transpose_w(3, w_grp23[:, 2:4, :, :])
                 quantize_w(1, 1, w_grp1)
                 quantize_w(2, 2, w_grp23)
-                interleave_y_gpsimd(2)
+                interleave_y(2, Y23_PIECES)
             if i == 10:
                 quantize_y(2)
-                interleave_y_gpsimd(3)
+                interleave_y(3, Y23_PIECES)
             if i == 16:
                 quantize_y(3)
             bank(order[i][0], order[i][1])

@@ -25,8 +25,9 @@ BN_EPS = 1e-5
 
 Y0_PIECES = (("v", 0, 256), ("v", 256, 384), ("s", 384, 512))
 Y1_PIECES = (("v", 0, 288), ("s", 288, 512))
-Y23_PIECES = (("v", 0, 320), ("s", 320, 512))
 SKEW = 3
+WARM = 4
+WARM2 = 4
 
 
 def bank_order():
@@ -58,6 +59,8 @@ def tile_nonlocalblocknd_pc_kernel(tc, y, w_w, w_b, bn_gamma, out_0, out_1, out_
         nc.scalar.dma_start(out=b_sb[:], in_=w_b.rearrange("(p m) -> p m", m=M_TILES))
         nc.scalar.dma_start(out=g_sb[:], in_=bn_gamma.rearrange("(p m) -> p m", m=M_TILES))
 
+        zeros = keep.tile([P, N_TILE], BF16, name="zeros")
+        nc.vector.memset(zeros[:], 0.0)
         one = keep.tile([P, 1], F32, name="one")
         junk = keep.tile([P, 1], F32, name="junk")
         nc.vector.memset(one[:], 1.0)
@@ -65,6 +68,10 @@ def tile_nonlocalblocknd_pc_kernel(tc, y, w_w, w_b, bn_gamma, out_0, out_1, out_
 
         ident = keep.tile([P, P], F32, name="ident")
         make_identity(nc, ident[:])
+
+        warm = psum.tile([P, N_TILE], F32, name="warm", tag="bank")
+        for i in range(WARM):
+            nc.tensor.matmul(warm[:], lhsT=zeros[:, 0:P], rhs=zeros[:], start=True, stop=True)
 
         w_raw = keep.tile([P, M_TILES, K], BF16, name="w_raw")
         y_raw = []
@@ -138,6 +145,7 @@ def tile_nonlocalblocknd_pc_kernel(tc, y, w_w, w_b, bn_gamma, out_0, out_1, out_
         mv = keep.tile([P, M_TILES, 2], F32, name="mv")
         res = {}
         seen = {}
+        pending = []
 
         def bank(m, j):
             h = j // 2
@@ -170,12 +178,18 @@ def tile_nonlocalblocknd_pc_kernel(tc, y, w_w, w_b, bn_gamma, out_0, out_1, out_
                 nc.sync.dma_start(out=o_v[:, m, j * N_TILE:(j + 1) * N_TILE], in_=r[:, e * N_TILE:(e + 1) * N_TILE])
             elif seen[(m, h)] == 2:
                 nc.sync.dma_start(out=o_v[:, m, 2 * h * N_TILE:2 * (h + 1) * N_TILE], in_=r[:])
+            for done_m in pending:
+                nc.vector.bn_aggr(out=mv[:, done_m, :], in_=stats[:, done_m, :, :].rearrange("p j s -> p (j s)"))
+            pending.clear()
             if seen[m] == CHUNKS:
-                nc.vector.bn_aggr(out=mv[:, m, :], in_=stats[:, m, :, :].rearrange("p j s -> p (j s)"))
+                pending.append(m)
 
         w_grp0 = keep.tile([P, 2, P, 2], F32, name="w_grp0", align_bytes=64)
         w_grp1 = keep.tile([P, 2, P, 2], F32, name="w_grp1", align_bytes=64)
         transpose_w(0, w_grp0[:])
+        warm2 = psum.tile([P, N_TILE], F32, name="warm2", tag="bank")
+        for i in range(WARM2):
+            nc.tensor.matmul(warm2[:], lhsT=zeros[:, 0:P], rhs=zeros[:], start=True, stop=True)
         interleave_y(0, Y0_PIECES)
         quantize_w(0, 1, w_grp0)
         quantize_y(0)
@@ -192,21 +206,23 @@ def tile_nonlocalblocknd_pc_kernel(tc, y, w_w, w_b, bn_gamma, out_0, out_1, out_
                 transpose_w(3, w_grp23[:, 2:4, :, :])
                 quantize_w(1, 1, w_grp1)
                 quantize_w(2, 2, w_grp23)
-                interleave_y(2, Y23_PIECES)
+                interleave_y_gpsimd(2)
             if i == 10:
                 quantize_y(2)
-                interleave_y(3, Y23_PIECES)
+                interleave_y_gpsimd(3)
             if i == 16:
                 quantize_y(3)
             bank(order[i][0], order[i][1])
+        for done_m in pending:
+            nc.vector.bn_aggr(out=mv[:, done_m, :], in_=stats[:, done_m, :, :].rearrange("p j s -> p (j s)"))
 
         sd = keep.tile([P, M_TILES], F32, name="sd")
         rs = keep.tile([P, M_TILES], F32, name="rs")
         gain = keep.tile([P, M_TILES], F32, name="gain")
         mean = keep.tile([P, M_TILES], F32, name="mean")
         nc.scalar.activation(out=sd[:], in_=mv[:, :, 1], func=ACT.Sqrt, bias=BN_EPS, scale=1.0)
+        nc.vector.tensor_add(out=mean[:], in0=mv[:, :, 0], in1=b_sb[:])
+        nc.scalar.dma_start(out=out_1.rearrange("(p m) -> p m", m=M_TILES), in_=mean[:])
         nc.vector.reciprocal(out=rs[:], in_=sd[:])
         nc.vector.tensor_mul(out=gain[:], in0=rs[:], in1=g_sb[:])
         nc.sync.dma_start(out=out_2.rearrange("(p m) -> p m", m=M_TILES), in_=gain[:])
-        nc.vector.tensor_add(out=mean[:], in0=mv[:, :, 0], in1=b_sb[:])
-        nc.scalar.dma_start(out=out_1.rearrange("(p m) -> p m", m=M_TILES), in_=mean[:])

@@ -56,8 +56,6 @@ def tile_nonlocalblocknd_pc_kernel(tc, y, w_w, w_b, bn_gamma, out_0, out_1, out_
 
         b_sb = keep.tile([P, M_TILES], BF16, name="b_sb")
         g_sb = keep.tile([P, M_TILES], BF16, name="g_sb")
-        nc.scalar.dma_start(out=b_sb[:], in_=w_b.rearrange("(p m) -> p m", m=M_TILES))
-        nc.scalar.dma_start(out=g_sb[:], in_=bn_gamma.rearrange("(p m) -> p m", m=M_TILES))
 
         zeros = keep.tile([P, N_TILE], BF16, name="zeros")
         nc.vector.memset(zeros[:], 0.0)
@@ -81,9 +79,11 @@ def tile_nonlocalblocknd_pc_kernel(tc, y, w_w, w_b, bn_gamma, out_0, out_1, out_
         nc.sync.dma_start(out=y_raw[0][:, :, 0:256], in_=y_v[:, :, 0:256])
         nc.sync.dma_start(out=y_raw[0][:, :, 256:512], in_=y_v[:, :, 256:512])
         nc.sync.dma_start(out=y_raw[1][:], in_=y_v[:, :, N_TILE:2 * N_TILE])
+        nc.sync.dma_start(out=b_sb[:], in_=w_b.rearrange("(p m) -> p m", m=M_TILES))
         nc.sync.dma_start(out=w_raw[:, 2:M_TILES, :], in_=w_v[:, 2:M_TILES, :])
         nc.sync.dma_start(out=y_raw[2][:], in_=y_v[:, :, 2 * N_TILE:3 * N_TILE])
         nc.sync.dma_start(out=y_raw[3][:], in_=y_v[:, :, 3 * N_TILE:4 * N_TILE])
+        nc.sync.dma_start(out=g_sb[:], in_=bn_gamma.rearrange("(p m) -> p m", m=M_TILES))
 
         y_grp = {}
         y_codes = {}
@@ -96,11 +96,12 @@ def tile_nonlocalblocknd_pc_kernel(tc, y, w_w, w_b, bn_gamma, out_0, out_1, out_
             grp = keep.tile([P, N_TILE, PACK], BF16, name="y_grp%d" % j, align_bytes=64)
             y_grp[j] = grp
             for eng, c0, c1 in pieces:
-                src = y_raw[j][:, :, c0:c1].rearrange("p t c -> p c t")
+                src = y_raw[j][:, :, c0:c1].rearrange("p t (c i) -> p c t i", i=4)
+                dst = grp[:, c0:c1, :].rearrange("p (c i) t -> p c t i", i=4)
                 if eng == "v":
-                    nc.vector.tensor_copy(out=grp[:, c0:c1, :], in_=src)
+                    nc.vector.tensor_copy(out=dst, in_=src)
                 else:
-                    nc.scalar.copy(out=grp[:, c0:c1, :], in_=src)
+                    nc.scalar.copy(out=dst, in_=src)
 
         def interleave_y_gpsimd(j):
             grp = keep.tile([P, N_TILE, PACK], BF16, name="y_grp%d" % j, tag="shared_grp", align_bytes=64)

@@ -27,7 +27,9 @@ Y0_PIECES = (("v", 0, 256), ("v", 256, 384), ("s", 384, 512))
 Y1_PIECES = (("v", 0, 288), ("s", 288, 512))
 SKEW = 3
 WARM = 4
-WARM2 = 4
+WARM2 = 3
+WARM_Y0 = 2
+WARM3 = 3
 
 
 def bank_order():
@@ -56,6 +58,8 @@ def tile_nonlocalblocknd_pc_kernel(tc, y, w_w, w_b, bn_gamma, out_0, out_1, out_
 
         b_sb = keep.tile([P, M_TILES], BF16, name="b_sb")
         g_sb = keep.tile([P, M_TILES], BF16, name="g_sb")
+        nc.scalar.dma_start(out=b_sb[:], in_=w_b.rearrange("(p m) -> p m", m=M_TILES))
+        nc.scalar.dma_start(out=g_sb[:], in_=bn_gamma.rearrange("(p m) -> p m", m=M_TILES))
 
         zeros = keep.tile([P, N_TILE], BF16, name="zeros")
         nc.vector.memset(zeros[:], 0.0)
@@ -79,11 +83,9 @@ def tile_nonlocalblocknd_pc_kernel(tc, y, w_w, w_b, bn_gamma, out_0, out_1, out_
         nc.sync.dma_start(out=y_raw[0][:, :, 0:256], in_=y_v[:, :, 0:256])
         nc.sync.dma_start(out=y_raw[0][:, :, 256:512], in_=y_v[:, :, 256:512])
         nc.sync.dma_start(out=y_raw[1][:], in_=y_v[:, :, N_TILE:2 * N_TILE])
-        nc.sync.dma_start(out=b_sb[:], in_=w_b.rearrange("(p m) -> p m", m=M_TILES))
         nc.sync.dma_start(out=w_raw[:, 2:M_TILES, :], in_=w_v[:, 2:M_TILES, :])
         nc.sync.dma_start(out=y_raw[2][:], in_=y_v[:, :, 2 * N_TILE:3 * N_TILE])
         nc.sync.dma_start(out=y_raw[3][:], in_=y_v[:, :, 3 * N_TILE:4 * N_TILE])
-        nc.sync.dma_start(out=g_sb[:], in_=bn_gamma.rearrange("(p m) -> p m", m=M_TILES))
 
         y_grp = {}
         y_codes = {}
@@ -96,12 +98,11 @@ def tile_nonlocalblocknd_pc_kernel(tc, y, w_w, w_b, bn_gamma, out_0, out_1, out_
             grp = keep.tile([P, N_TILE, PACK], BF16, name="y_grp%d" % j, align_bytes=64)
             y_grp[j] = grp
             for eng, c0, c1 in pieces:
-                src = y_raw[j][:, :, c0:c1].rearrange("p t (c i) -> p c t i", i=4)
-                dst = grp[:, c0:c1, :].rearrange("p (c i) t -> p c t i", i=4)
+                src = y_raw[j][:, :, c0:c1].rearrange("p t c -> p c t")
                 if eng == "v":
-                    nc.vector.tensor_copy(out=dst, in_=src)
+                    nc.vector.tensor_copy(out=grp[:, c0:c1, :], in_=src)
                 else:
-                    nc.scalar.copy(out=dst, in_=src)
+                    nc.scalar.copy(out=grp[:, c0:c1, :], in_=src)
 
         def interleave_y_gpsimd(j):
             grp = keep.tile([P, N_TILE, PACK], BF16, name="y_grp%d" % j, tag="shared_grp", align_bytes=64)
@@ -191,6 +192,9 @@ def tile_nonlocalblocknd_pc_kernel(tc, y, w_w, w_b, bn_gamma, out_0, out_1, out_
         warm2 = psum.tile([P, N_TILE], F32, name="warm2", tag="bank")
         for i in range(WARM2):
             nc.tensor.matmul(warm2[:], lhsT=zeros[:, 0:P], rhs=zeros[:], start=True, stop=True)
+        warm_y0 = psum.tile([P, N_TILE], F32, name="warm_y0", tag="bank")
+        for i in range(WARM_Y0):
+            nc.tensor.matmul(warm_y0[:], lhsT=zeros[:, 0:P], rhs=y_raw[0][:, 0, :], start=True, stop=True)
         interleave_y(0, Y0_PIECES)
         quantize_w(0, 1, w_grp0)
         quantize_y(0)
@@ -205,6 +209,9 @@ def tile_nonlocalblocknd_pc_kernel(tc, y, w_w, w_b, bn_gamma, out_0, out_1, out_
                 transpose_w(2, w_grp23[:, 0:2, :, :])
             if i == 3:
                 transpose_w(3, w_grp23[:, 2:4, :, :])
+                warm3 = psum.tile([P, N_TILE], F32, name="warm3", tag="bank")
+                for d in range(WARM3):
+                    nc.tensor.matmul(warm3[:], lhsT=zeros[:, 0:P], rhs=zeros[:], start=True, stop=True)
                 quantize_w(1, 1, w_grp1)
                 quantize_w(2, 2, w_grp23)
                 interleave_y_gpsimd(2)

@@ -23,26 +23,12 @@ N_TILE = 512
 CHUNKS = N // N_TILE
 BN_EPS = 1e-5
 
-Y0_PIECES = (("v", 0, 256), ("v", 256, 384), ("s", 384, 512))
-Y1_PIECES = (("v", 0, 288), ("s", 288, 512))
-SKEW = 3
+Y0_PIECES = (("v", 0, 256), ("v", 256, 512))
 WARM = 4
 WARM2 = 3
-WARM_Y0 = 2
-WARM3 = 3
-
-
-def bank_order():
-    order = [(0, 0), (1, 0), (0, 1), (1, 1)]
-    for m in range(2, M_TILES):
-        order.extend([(m, 0), (m, 1)])
-    for m in range(SKEW):
-        order.append((m, 2))
-    for m in range(SKEW):
-        order.append((m, 3))
-    for m in range(SKEW, M_TILES):
-        order.extend([(m, 2), (m, 3)])
-    return order
+S_LAST = 2
+QUANT_FIRST = 4
+QUANT_STEP = 6
 
 
 def tile_nonlocalblocknd_pc_kernel(tc, y, w_w, w_b, bn_gamma, out_0, out_1, out_2):
@@ -71,9 +57,12 @@ def tile_nonlocalblocknd_pc_kernel(tc, y, w_w, w_b, bn_gamma, out_0, out_1, out_
         ident = keep.tile([P, P], F32, name="ident")
         make_identity(nc, ident[:])
 
-        warm = psum.tile([P, N_TILE], F32, name="warm", tag="bank")
-        for i in range(WARM):
-            nc.tensor.matmul(warm[:], lhsT=zeros[:, 0:P], rhs=zeros[:], start=True, stop=True)
+        def dummies(count, name):
+            warm = psum.tile([P, N_TILE], F32, name=name, tag="bank")
+            for i in range(count):
+                nc.tensor.matmul(warm[:], lhsT=zeros[:, 0:P], rhs=zeros[:], start=True, stop=True)
+
+        dummies(WARM, "warm")
 
         w_raw = keep.tile([P, M_TILES, K], BF16, name="w_raw")
         y_raw = []
@@ -82,10 +71,10 @@ def tile_nonlocalblocknd_pc_kernel(tc, y, w_w, w_b, bn_gamma, out_0, out_1, out_
         nc.sync.dma_start(out=w_raw[:, 0:2, :], in_=w_v[:, 0:2, :])
         nc.sync.dma_start(out=y_raw[0][:, :, 0:256], in_=y_v[:, :, 0:256])
         nc.sync.dma_start(out=y_raw[0][:, :, 256:512], in_=y_v[:, :, 256:512])
-        nc.sync.dma_start(out=y_raw[1][:], in_=y_v[:, :, N_TILE:2 * N_TILE])
-        nc.sync.dma_start(out=w_raw[:, 2:M_TILES, :], in_=w_v[:, 2:M_TILES, :])
-        nc.sync.dma_start(out=y_raw[2][:], in_=y_v[:, :, 2 * N_TILE:3 * N_TILE])
-        nc.sync.dma_start(out=y_raw[3][:], in_=y_v[:, :, 3 * N_TILE:4 * N_TILE])
+        nc.sync.dma_start(out=w_raw[:, 2:4, :], in_=w_v[:, 2:4, :])
+        nc.sync.dma_start(out=w_raw[:, 4:8, :], in_=w_v[:, 4:8, :])
+        for j in range(1, CHUNKS):
+            nc.sync.dma_start(out=y_raw[j][:], in_=y_v[:, :, j * N_TILE:(j + 1) * N_TILE])
 
         y_grp = {}
         y_codes = {}
@@ -127,13 +116,16 @@ def tile_nonlocalblocknd_pc_kernel(tc, y, w_w, w_b, bn_gamma, out_0, out_1, out_
                 in_=y_grp[j][:].rearrange("p c t -> p (c t)"),
             )
 
-        def transpose_w(q, grp_half):
+        def transpose_w(q, grp_half, eng):
             wt = psum.tile([P, 2, 2, P], F32, name="wt", tag="bank")
             for mm in range(2):
                 for u in range(2):
                     base = 256 * (2 * q + mm)
                     nc.tensor.transpose(wt[:, mm, u, :], w_words[:, base + u:base + 256:2], ident[:])
-            nc.scalar.copy(out=grp_half, in_=wt[:].rearrange("p m u r -> p m r u"))
+            if eng == "s":
+                nc.scalar.copy(out=grp_half, in_=wt[:].rearrange("p m u r -> p m r u"))
+            else:
+                nc.vector.tensor_copy(out=grp_half, in_=wt[:].rearrange("p m u r -> p m r u"))
 
         def quantize_w(q0, pairs, grp):
             cols = slice(2 * P * q0, 2 * P * (q0 + pairs))
@@ -143,19 +135,20 @@ def tile_nonlocalblocknd_pc_kernel(tc, y, w_w, w_b, bn_gamma, out_0, out_1, out_
                 in_=grp[:].rearrange("p m r u -> p (m r u)").bitcast(BF16),
             )
 
-        stats = keep.tile([P, M_TILES, CHUNKS, 6], F32, name="stats")
+        stats = keep.tile([P, M_TILES, CHUNKS * 6], F32, name="stats")
         mv = keep.tile([P, M_TILES, 2], F32, name="mv")
-        res = {}
-        seen = {}
+        res = []
+        for m in range(M_TILES):
+            res.append(keep.tile([P, N], F32, name="res%d" % m))
         pending = []
+        neg_b = keep.tile([P, M_TILES], F32, name="neg_b")
+        sums = keep.tile([P, M_TILES], F32, name="sums")
+        scrap = keep.tile([P, N_TILE], F32, name="scrap")
+        late = []
 
-        def bank(m, j):
-            h = j // 2
-            e = j % 2
-            if (m, h) not in res:
-                res[(m, h)] = keep.tile([P, 2 * N_TILE], F32, name="res%d_%d" % (m, h))
-            r = res[(m, h)]
+        def bank(m, j, scalar_stats=False):
             cols = slice(P * m, P * (m + 1))
+            span = slice(j * N_TILE, (j + 1) * N_TILE)
             acc = psum.tile([P, N_TILE], F32, name="acc", tag="bank")
             nc.tensor.matmul_mx(
                 out=acc[:],
@@ -166,63 +159,53 @@ def tile_nonlocalblocknd_pc_kernel(tc, y, w_w, w_b, bn_gamma, out_0, out_1, out_
                 start=True,
                 stop=True,
             )
-            nc.scalar.activation(
-                out=r[:, e * N_TILE:(e + 1) * N_TILE],
-                in_=acc[:],
-                func=ACT.Identity,
-                bias=b_sb[:, m:m + 1],
-                scale=1.0,
-            )
-            nc.vector.bn_stats(out=stats[:, m, j, :], in_=acc[:])
-            seen[(m, h)] = seen.get((m, h), 0) + 1
-            seen[m] = seen.get(m, 0) + 1
-            if (m, h) == (M_TILES - 1, 1):
-                nc.sync.dma_start(out=o_v[:, m, j * N_TILE:(j + 1) * N_TILE], in_=r[:, e * N_TILE:(e + 1) * N_TILE])
-            elif seen[(m, h)] == 2:
-                nc.sync.dma_start(out=o_v[:, m, 2 * h * N_TILE:2 * (h + 1) * N_TILE], in_=r[:])
+            if scalar_stats:
+                nc.scalar.activation(out=res[m][:, span], in_=acc[:], func=ACT.Identity, bias=b_sb[:, m:m + 1], scale=1.0,
+                                     accum_out=sums[:, m:m + 1])
+                late.append((m, acc))
+            else:
+                nc.scalar.activation(out=res[m][:, span], in_=acc[:], func=ACT.Identity, bias=b_sb[:, m:m + 1], scale=1.0)
+                nc.vector.bn_stats(out=stats[:, m, 6 * j:6 * (j + 1)], in_=acc[:])
+            nc.sync.dma_start(out=o_v[:, m, span], in_=res[m][:, span])
             for done_m in pending:
-                nc.vector.bn_aggr(out=mv[:, done_m, :], in_=stats[:, done_m, :, :].rearrange("p j s -> p (j s)"))
+                nc.vector.bn_aggr(out=mv[:, done_m, :], in_=stats[:, done_m, :])
             pending.clear()
-            if seen[m] == CHUNKS:
+            if j == CHUNKS - 1 and not scalar_stats:
                 pending.append(m)
+
+        nc.vector.tensor_scalar(out=neg_b[:], in0=b_sb[:], scalar1=-1.0, scalar2=None, op0=ALU.mult)
+        nc.vector.memset(stats[:, M_TILES - S_LAST:M_TILES, 18:19], float(N_TILE))
 
         w_grp0 = keep.tile([P, 2, P, 2], F32, name="w_grp0", align_bytes=64)
         w_grp1 = keep.tile([P, 2, P, 2], F32, name="w_grp1", align_bytes=64)
-        transpose_w(0, w_grp0[:])
-        warm2 = psum.tile([P, N_TILE], F32, name="warm2", tag="bank")
-        for i in range(WARM2):
-            nc.tensor.matmul(warm2[:], lhsT=zeros[:, 0:P], rhs=zeros[:], start=True, stop=True)
-        warm_y0 = psum.tile([P, N_TILE], F32, name="warm_y0", tag="bank")
-        for i in range(WARM_Y0):
-            nc.tensor.matmul(warm_y0[:], lhsT=zeros[:, 0:P], rhs=y_raw[0][:, 0, :], start=True, stop=True)
+        w_grp23 = keep.tile([P, 4, P, 2], F32, name="w_grp23", tag="shared_grp", align_bytes=64)
+        transpose_w(0, w_grp0[:], "s")
+        dummies(WARM2, "warm2")
         interleave_y(0, Y0_PIECES)
         quantize_w(0, 1, w_grp0)
         quantize_y(0)
-        interleave_y(1, Y1_PIECES)
-        quantize_y(1)
-
-        order = bank_order()
+        transpose_w(1, w_grp1[:], "s")
+        transpose_w(2, w_grp23[:, 0:2, :, :], "s")
+        transpose_w(3, w_grp23[:, 2:4, :, :], "s")
+        quantize_w(1, 1, w_grp1)
+        quantize_w(2, 2, w_grp23)
+        interleave_y_gpsimd(1)
+        order = [(m, j) for j in range(CHUNKS) for m in range(M_TILES)]
         for i in range(len(order)):
-            if i == 2:
-                transpose_w(1, w_grp1[:])
-                w_grp23 = keep.tile([P, 4, P, 2], F32, name="w_grp23", tag="shared_grp", align_bytes=64)
-                transpose_w(2, w_grp23[:, 0:2, :, :])
-            if i == 3:
-                transpose_w(3, w_grp23[:, 2:4, :, :])
-                warm3 = psum.tile([P, N_TILE], F32, name="warm3", tag="bank")
-                for d in range(WARM3):
-                    nc.tensor.matmul(warm3[:], lhsT=zeros[:, 0:P], rhs=zeros[:], start=True, stop=True)
-                quantize_w(1, 1, w_grp1)
-                quantize_w(2, 2, w_grp23)
-                interleave_y_gpsimd(2)
-            if i == 10:
-                quantize_y(2)
-                interleave_y_gpsimd(3)
-            if i == 16:
-                quantize_y(3)
-            bank(order[i][0], order[i][1])
+            bank(order[i][0], order[i][1], i >= len(order) - S_LAST)
+            for c in range(1, CHUNKS):
+                if i == QUANT_FIRST + QUANT_STEP * (c - 1):
+                    quantize_y(c)
+                    if c + 1 < CHUNKS:
+                        interleave_y_gpsimd(c + 1)
         for done_m in pending:
-            nc.vector.bn_aggr(out=mv[:, done_m, :], in_=stats[:, done_m, :, :].rearrange("p j s -> p (j s)"))
+            nc.vector.bn_aggr(out=mv[:, done_m, :], in_=stats[:, done_m, :])
+        for m, acc in late:
+            nc.scalar.activation(out=stats[:, m, 19:20], in_=sums[:, m:m + 1], func=ACT.Identity, bias=neg_b[:, m:m + 1], scale=1.0 / N_TILE)
+        for m, acc in late:
+            nc.scalar.activation(out=scrap[:], in_=acc[:], func=ACT.Square, bias=stats[:, m, 19:20], scale=-1.0,
+                                 accum_out=stats[:, m, 20:21])
+            nc.vector.bn_aggr(out=mv[:, m, :], in_=stats[:, m, 0:21])
 
         sd = keep.tile([P, M_TILES], F32, name="sd")
         rs = keep.tile([P, M_TILES], F32, name="rs")

@@ -52,7 +52,7 @@ def tile_nonlocalblocknd_pc_kernel(tc, y, w_w, w_b, bn_gamma, out_0, out_1, out_
         one = keep.tile([P, 1], F32, name="one")
         junk = keep.tile([P, 1], F32, name="junk")
         nc.vector.memset(one[:], 1.0)
-        nc.scalar.activation(out=junk[:], in_=one[:], func=ACT.Sqrt)
+        nc.scalar.activation(out=junk[:], in_=one[:], func=ACT.Abs_reciprocal_sqrt)
 
         ident = keep.tile([P, P], F32, name="ident")
         make_identity(nc, ident[:])
@@ -72,7 +72,8 @@ def tile_nonlocalblocknd_pc_kernel(tc, y, w_w, w_b, bn_gamma, out_0, out_1, out_
         nc.sync.dma_start(out=y_raw[0][:, :, 0:256], in_=y_v[:, :, 0:256])
         nc.sync.dma_start(out=y_raw[0][:, :, 256:512], in_=y_v[:, :, 256:512])
         nc.sync.dma_start(out=w_raw[:, 2:4, :], in_=w_v[:, 2:4, :])
-        nc.sync.dma_start(out=w_raw[:, 4:8, :], in_=w_v[:, 4:8, :])
+        nc.sync.dma_start(out=w_raw[:, 4:6, :], in_=w_v[:, 4:6, :])
+        nc.sync.dma_start(out=w_raw[:, 6:8, :], in_=w_v[:, 6:8, :])
         for j in range(1, CHUNKS):
             nc.sync.dma_start(out=y_raw[j][:], in_=y_v[:, :, j * N_TILE:(j + 1) * N_TILE])
 
@@ -207,13 +208,11 @@ def tile_nonlocalblocknd_pc_kernel(tc, y, w_w, w_b, bn_gamma, out_0, out_1, out_
                                  accum_out=stats[:, m, 20:21])
             nc.vector.bn_aggr(out=mv[:, m, :], in_=stats[:, m, 0:21])
 
-        sd = keep.tile([P, M_TILES], F32, name="sd")
         rs = keep.tile([P, M_TILES], F32, name="rs")
         gain = keep.tile([P, M_TILES], F32, name="gain")
         mean = keep.tile([P, M_TILES], F32, name="mean")
-        nc.scalar.activation(out=sd[:], in_=mv[:, :, 1], func=ACT.Sqrt, bias=BN_EPS, scale=1.0)
+        nc.scalar.activation(out=rs[:], in_=mv[:, :, 1], func=ACT.Abs_reciprocal_sqrt, bias=BN_EPS, scale=1.0)
         nc.vector.tensor_add(out=mean[:], in0=mv[:, :, 0], in1=b_sb[:])
         nc.scalar.dma_start(out=out_1.rearrange("(p m) -> p m", m=M_TILES), in_=mean[:])
-        nc.vector.reciprocal(out=rs[:], in_=sd[:])
         nc.vector.tensor_mul(out=gain[:], in0=rs[:], in1=g_sb[:])
         nc.sync.dma_start(out=out_2.rearrange("(p m) -> p m", m=M_TILES), in_=gain[:])

@@ -27,8 +27,8 @@ Y0_PIECES = (("v", 0, 256), ("v", 256, 512))
 WARM = 4
 WARM2 = 3
 S_LAST = 2
-QUANT_FIRST = 4
-QUANT_STEP = 6
+Y1_V = 256
+QUANT_AT = {1: 3, 2: 9, 3: 15}
 
 
 def tile_nonlocalblocknd_pc_kernel(tc, y, w_w, w_b, bn_gamma, out_0, out_1, out_2):
@@ -94,27 +94,28 @@ def tile_nonlocalblocknd_pc_kernel(tc, y, w_w, w_b, bn_gamma, out_0, out_1, out_
                 else:
                     nc.scalar.copy(out=grp[:, c0:c1, :], in_=src)
 
-        def interleave_y_gpsimd(j):
-            grp = keep.tile([P, N_TILE, PACK], BF16, name="y_grp%d" % j, tag="shared_grp", align_bytes=64)
+        def interleave_y_gpsimd(j, c0=0):
+            grp = keep.tile([P, N_TILE - c0, PACK], BF16, name="y_grp%d" % j, tag="shared_grp", align_bytes=64)
             y_grp[j] = grp
             nc.gpsimd.tensor_scalar(
                 out=grp[:],
-                in0=y_raw[j][:].rearrange("p t c -> p c t"),
+                in0=y_raw[j][:, :, c0:N_TILE].rearrange("p t c -> p c t"),
                 scalar1=1.0,
                 scalar2=0.0,
                 op0=ALU.mult,
                 op1=ALU.add,
             )
 
-        def quantize_y(j):
-            codes = keep.tile([P, N_TILE], U32, name="y_codes%d" % j, align_bytes=64)
-            scales = keep.tile([P, N_TILE], U8, name="y_scales%d" % j, align_bytes=64)
-            y_codes[j] = codes
-            y_scales[j] = scales
+        def quantize_y(j, c0=0, c1=N_TILE, grp=None):
+            if j not in y_codes:
+                y_codes[j] = keep.tile([P, N_TILE], U32, name="y_codes%d" % j, align_bytes=64)
+                y_scales[j] = keep.tile([P, N_TILE], U8, name="y_scales%d" % j, align_bytes=64)
+            if grp is None:
+                grp = y_grp[j]
             nc.vector.quantize_mx(
-                out=codes[:].bitcast(FP8X4),
-                scales=scales[:],
-                in_=y_grp[j][:].rearrange("p c t -> p (c t)"),
+                out=y_codes[j][:, c0:c1].bitcast(FP8X4),
+                scales=y_scales[j][:, c0:c1],
+                in_=grp[:].rearrange("p c t -> p (c t)"),
             )
 
         def transpose_w(q, grp_half, eng):
@@ -142,7 +143,6 @@ def tile_nonlocalblocknd_pc_kernel(tc, y, w_w, w_b, bn_gamma, out_0, out_1, out_
         for m in range(M_TILES):
             res.append(keep.tile([P, N], F32, name="res%d" % m))
         pending = []
-        neg_b = keep.tile([P, M_TILES], F32, name="neg_b")
         sums = keep.tile([P, M_TILES], F32, name="sums")
         scrap = keep.tile([P, N_TILE], F32, name="scrap")
         late = []
@@ -163,10 +163,10 @@ def tile_nonlocalblocknd_pc_kernel(tc, y, w_w, w_b, bn_gamma, out_0, out_1, out_
             if scalar_stats:
                 nc.scalar.activation(out=res[m][:, span], in_=acc[:], func=ACT.Identity, bias=b_sb[:, m:m + 1], scale=1.0,
                                      accum_out=sums[:, m:m + 1])
-                late.append((m, acc))
+                late.append((m, span))
             else:
                 nc.scalar.activation(out=res[m][:, span], in_=acc[:], func=ACT.Identity, bias=b_sb[:, m:m + 1], scale=1.0)
-                nc.vector.bn_stats(out=stats[:, m, 6 * j:6 * (j + 1)], in_=acc[:])
+                nc.vector.bn_stats(out=stats[:, m, 6 * j:6 * (j + 1)], in_=res[m][:, span])
             nc.sync.dma_start(out=o_v[:, m, span], in_=res[m][:, span])
             for done_m in pending:
                 nc.vector.bn_aggr(out=mv[:, done_m, :], in_=stats[:, done_m, :])
@@ -174,7 +174,6 @@ def tile_nonlocalblocknd_pc_kernel(tc, y, w_w, w_b, bn_gamma, out_0, out_1, out_
             if j == CHUNKS - 1 and not scalar_stats:
                 pending.append(m)
 
-        nc.vector.tensor_scalar(out=neg_b[:], in0=b_sb[:], scalar1=-1.0, scalar2=None, op0=ALU.mult)
         nc.vector.memset(stats[:, M_TILES - S_LAST:M_TILES, 18:19], float(N_TILE))
 
         w_grp0 = keep.tile([P, 2, P, 2], F32, name="w_grp0", align_bytes=64)
@@ -189,22 +188,28 @@ def tile_nonlocalblocknd_pc_kernel(tc, y, w_w, w_b, bn_gamma, out_0, out_1, out_
         transpose_w(2, w_grp23[:, 0:2, :, :], "s")
         transpose_w(3, w_grp23[:, 2:4, :, :], "s")
         quantize_w(1, 1, w_grp1)
+        y1_head = keep.tile([P, Y1_V, PACK], BF16, name="y1_head", align_bytes=64)
+        nc.vector.tensor_copy(out=y1_head[:], in_=y_raw[1][:, :, 0:Y1_V].rearrange("p t c -> p c t"))
         quantize_w(2, 2, w_grp23)
-        interleave_y_gpsimd(1)
+        interleave_y_gpsimd(1, Y1_V)
+        quantize_y(1, 0, Y1_V, y1_head)
         order = [(m, j) for j in range(CHUNKS) for m in range(M_TILES)]
         for i in range(len(order)):
             bank(order[i][0], order[i][1], i >= len(order) - S_LAST)
             for c in range(1, CHUNKS):
-                if i == QUANT_FIRST + QUANT_STEP * (c - 1):
-                    quantize_y(c)
+                if i == QUANT_AT[c]:
+                    if c == 1:
+                        quantize_y(c, Y1_V, N_TILE)
+                    else:
+                        quantize_y(c)
                     if c + 1 < CHUNKS:
                         interleave_y_gpsimd(c + 1)
         for done_m in pending:
             nc.vector.bn_aggr(out=mv[:, done_m, :], in_=stats[:, done_m, :])
-        for m, acc in late:
-            nc.scalar.activation(out=stats[:, m, 19:20], in_=sums[:, m:m + 1], func=ACT.Identity, bias=neg_b[:, m:m + 1], scale=1.0 / N_TILE)
-        for m, acc in late:
-            nc.scalar.activation(out=scrap[:], in_=acc[:], func=ACT.Square, bias=stats[:, m, 19:20], scale=-1.0,
+        for m, span in late:
+            nc.scalar.mul(out=stats[:, m, 19:20], in_=sums[:, m:m + 1], mul=1.0 / N_TILE)
+        for m, span in late:
+            nc.scalar.activation(out=scrap[:], in_=res[m][:, span], func=ACT.Square, bias=stats[:, m, 19:20], scale=-1.0,
                                  accum_out=stats[:, m, 20:21])
             nc.vector.bn_aggr(out=mv[:, m, :], in_=stats[:, m, 0:21])
 
@@ -212,7 +217,7 @@ def tile_nonlocalblocknd_pc_kernel(tc, y, w_w, w_b, bn_gamma, out_0, out_1, out_
         gain = keep.tile([P, M_TILES], F32, name="gain")
         mean = keep.tile([P, M_TILES], F32, name="mean")
         nc.scalar.activation(out=rs[:], in_=mv[:, :, 1], func=ACT.Abs_reciprocal_sqrt, bias=BN_EPS, scale=1.0)
-        nc.vector.tensor_add(out=mean[:], in0=mv[:, :, 0], in1=b_sb[:])
+        nc.vector.tensor_copy(out=mean[:], in_=mv[:, :, 0])
         nc.scalar.dma_start(out=out_1.rearrange("(p m) -> p m", m=M_TILES), in_=mean[:])
         nc.vector.tensor_mul(out=gain[:], in0=rs[:], in1=g_sb[:])
         nc.sync.dma_start(out=out_2.rearrange("(p m) -> p m", m=M_TILES), in_=gain[:])

@@ -28,7 +28,7 @@ WARM = 4
 WARM2 = 3
 S_LAST = 2
 Y1_V = 256
-QUANT_AT = {1: 3, 2: 9, 3: 15}
+QUANT_AT = {1: 2, 2: 9, 3: 16}
 
 
 def tile_nonlocalblocknd_pc_kernel(tc, y, w_w, w_b, bn_gamma, out_0, out_1, out_2):

@@ -27,6 +27,7 @@ Y0_PIECES = (("v", 0, 256), ("v", 256, 512))
 WARM = 4
 WARM2 = 3
 S_LAST = 2
+S_COLS = 4
 Y1_V = 256
 QUANT_AT = {1: 2, 2: 9, 3: 16}
 
@@ -144,10 +145,16 @@ def tile_nonlocalblocknd_pc_kernel(tc, y, w_w, w_b, bn_gamma, out_0, out_1, out_
             res.append(keep.tile([P, N], F32, name="res%d" % m))
         pending = []
         sums = keep.tile([P, M_TILES], F32, name="sums")
-        scrap = keep.tile([P, N_TILE], F32, name="scrap")
+        dev2 = keep.tile([P, M_TILES], F32, name="dev2")
+        g32 = keep.tile([P, M_TILES], F32, name="g32")
+        ones = keep.tile([P, S_LAST], F32, name="ones")
+        rs = keep.tile([P, M_TILES], F32, name="rs")
+        gain = keep.tile([P, M_TILES], F32, name="gain")
+        mean = keep.tile([P, M_TILES], F32, name="mean")
         late = []
+        held = []
 
-        def bank(m, j, scalar_stats=False):
+        def bank(m, j, scalar_stats=False, hold_vector=False):
             cols = slice(P * m, P * (m + 1))
             span = slice(j * N_TILE, (j + 1) * N_TILE)
             acc = psum.tile([P, N_TILE], F32, name="acc", tag="bank")
@@ -166,15 +173,22 @@ def tile_nonlocalblocknd_pc_kernel(tc, y, w_w, w_b, bn_gamma, out_0, out_1, out_
                 late.append((m, span))
             else:
                 nc.scalar.activation(out=res[m][:, span], in_=acc[:], func=ACT.Identity, bias=b_sb[:, m:m + 1], scale=1.0)
-                nc.vector.bn_stats(out=stats[:, m, 6 * j:6 * (j + 1)], in_=res[m][:, span])
+                if hold_vector:
+                    held.append(lambda: nc.vector.bn_stats(out=stats[:, m, 6 * j:6 * (j + 1)], in_=res[m][:, span]))
+                else:
+                    nc.vector.bn_stats(out=stats[:, m, 6 * j:6 * (j + 1)], in_=res[m][:, span])
             nc.sync.dma_start(out=o_v[:, m, span], in_=res[m][:, span])
-            for done_m in pending:
-                nc.vector.bn_aggr(out=mv[:, done_m, :], in_=stats[:, done_m, :])
-            pending.clear()
+            if not scalar_stats and not hold_vector:
+                for done_m in pending:
+                    nc.vector.bn_aggr(out=mv[:, done_m, :], in_=stats[:, done_m, :])
+                pending.clear()
             if j == CHUNKS - 1 and not scalar_stats:
                 pending.append(m)
 
         nc.vector.memset(stats[:, M_TILES - S_LAST:M_TILES, 18:19], float(N_TILE))
+        nc.vector.memset(ones[:], 1.0)
+        nc.vector.tensor_scalar(out=stats[:, M_TILES - S_LAST:M_TILES, 20], in0=ones[:], scalar1=N * BN_EPS, scalar2=None, op0=ALU.mult)
+        nc.vector.tensor_copy(out=g32[:], in_=g_sb[:])
 
         w_grp0 = keep.tile([P, 2, P, 2], F32, name="w_grp0", align_bytes=64)
         w_grp1 = keep.tile([P, 2, P, 2], F32, name="w_grp1", align_bytes=64)
@@ -195,7 +209,7 @@ def tile_nonlocalblocknd_pc_kernel(tc, y, w_w, w_b, bn_gamma, out_0, out_1, out_
         quantize_y(1, 0, Y1_V, y1_head)
         order = [(m, j) for j in range(CHUNKS) for m in range(M_TILES)]
         for i in range(len(order)):
-            bank(order[i][0], order[i][1], i >= len(order) - S_LAST)
+            bank(order[i][0], order[i][1], i >= len(order) - S_LAST, i == len(order) - S_LAST - 1)
             for c in range(1, CHUNKS):
                 if i == QUANT_AT[c]:
                     if c == 1:
@@ -204,20 +218,32 @@ def tile_nonlocalblocknd_pc_kernel(tc, y, w_w, w_b, bn_gamma, out_0, out_1, out_
                         quantize_y(c)
                     if c + 1 < CHUNKS:
                         interleave_y_gpsimd(c + 1)
-        for done_m in pending:
-            nc.vector.bn_aggr(out=mv[:, done_m, :], in_=stats[:, done_m, :])
+        first_s = M_TILES - S_LAST
+        first_c = M_TILES - S_COLS
         for m, span in late:
             nc.scalar.mul(out=stats[:, m, 19:20], in_=sums[:, m:m + 1], mul=1.0 / N_TILE)
         for m, span in late:
-            nc.scalar.activation(out=scrap[:], in_=res[m][:, span], func=ACT.Square, bias=stats[:, m, 19:20], scale=-1.0,
-                                 accum_out=stats[:, m, 20:21])
             nc.vector.bn_aggr(out=mv[:, m, :], in_=stats[:, m, 0:21])
-
-        rs = keep.tile([P, M_TILES], F32, name="rs")
-        gain = keep.tile([P, M_TILES], F32, name="gain")
-        mean = keep.tile([P, M_TILES], F32, name="mean")
-        nc.scalar.activation(out=rs[:], in_=mv[:, :, 1], func=ACT.Abs_reciprocal_sqrt, bias=BN_EPS, scale=1.0)
+        for v_step in held:
+            v_step()
+        for done_m in pending:
+            nc.vector.bn_aggr(out=mv[:, done_m, :], in_=stats[:, done_m, :])
+        for m, span in late:
+            scrap = keep.tile([P, N_TILE], F32, name="scrap%d" % m)
+            nc.scalar.activation(out=scrap[:], in_=res[m][:, span], func=ACT.Square, bias=stats[:, m, 19:20], scale=-1.0,
+                                 accum_out=dev2[:, m:m + 1])
+            if m == first_s:
+                nc.scalar.activation(out=rs[:, 0:first_c], in_=mv[:, 0:first_c, 1], func=ACT.Abs_reciprocal_sqrt, bias=BN_EPS, scale=1.0)
+        for m, span in late:
+            nc.scalar.activation(out=rs[:, m:m + 1], in_=dev2[:, m:m + 1], func=ACT.Abs_reciprocal_sqrt, bias=mv[:, m, 1:2], scale=1.0 / N)
+        for m in range(first_c, first_s - 1):
+            nc.scalar.activation(out=rs[:, m:m + 1], in_=mv[:, m, 1:2], func=ACT.Abs_reciprocal_sqrt, bias=BN_EPS, scale=1.0)
+        for m in list(range(first_s, M_TILES)) + list(range(first_c, first_s - 1)):
+            nc.scalar.activation(out=gain[:, m:m + 1], in_=rs[:, m:m + 1], func=ACT.Copy, scale=g32[:, m:m + 1])
+        m = first_s - 1
+        nc.scalar.activation(out=rs[:, m:m + 1], in_=mv[:, m, 1:2], func=ACT.Abs_reciprocal_sqrt, bias=BN_EPS, scale=1.0)
+        nc.scalar.activation(out=gain[:, m:m + 1], in_=rs[:, m:m + 1], func=ACT.Copy, scale=g32[:, m:m + 1])
+        nc.vector.tensor_mul(out=gain[:, 0:first_c], in0=rs[:, 0:first_c], in1=g_sb[:, 0:first_c])
+        nc.scalar.dma_start(out=out_2.rearrange("(p m) -> p m", m=M_TILES), in_=gain[:])
         nc.vector.tensor_copy(out=mean[:], in_=mv[:, :, 0])
-        nc.scalar.dma_start(out=out_1.rearrange("(p m) -> p m", m=M_TILES), in_=mean[:])
-        nc.vector.tensor_mul(out=gain[:], in0=rs[:], in1=g_sb[:])
-        nc.sync.dma_start(out=out_2.rearrange("(p m) -> p m", m=M_TILES), in_=gain[:])
+        nc.sync.dma_start(out=out_1.rearrange("(p m) -> p m", m=M_TILES), in_=mean[:])

@@ -23,13 +23,13 @@ N_TILE = 512
 CHUNKS = N // N_TILE
 BN_EPS = 1e-5
 
-Y0_PIECES = (("v", 0, 256), ("v", 256, 512))
 WARM = 4
 WARM2 = 3
 S_LAST = 2
-S_COLS = 4
+Y0_S = 512
 Y1_V = 256
-QUANT_AT = {1: 2, 2: 9, 3: 16}
+W3_E = "s"
+W2_E = "s"
 
 
 def tile_nonlocalblocknd_pc_kernel(tc, y, w_w, w_b, bn_gamma, out_0, out_1, out_2):
@@ -69,81 +69,89 @@ def tile_nonlocalblocknd_pc_kernel(tc, y, w_w, w_b, bn_gamma, out_0, out_1, out_
         y_raw = []
         for j in range(CHUNKS):
             y_raw.append(keep.tile([P, PACK, N_TILE], BF16, name="y_raw%d" % j))
-        nc.sync.dma_start(out=w_raw[:, 0:2, :], in_=w_v[:, 0:2, :])
-        nc.sync.dma_start(out=y_raw[0][:, :, 0:256], in_=y_v[:, :, 0:256])
-        nc.sync.dma_start(out=y_raw[0][:, :, 256:512], in_=y_v[:, :, 256:512])
-        nc.sync.dma_start(out=w_raw[:, 2:4, :], in_=w_v[:, 2:4, :])
-        nc.sync.dma_start(out=w_raw[:, 4:6, :], in_=w_v[:, 4:6, :])
-        nc.sync.dma_start(out=w_raw[:, 6:8, :], in_=w_v[:, 6:8, :])
-        for j in range(1, CHUNKS):
-            nc.sync.dma_start(out=y_raw[j][:], in_=y_v[:, :, j * N_TILE:(j + 1) * N_TILE])
 
-        y_grp = {}
-        y_codes = {}
-        y_scales = {}
+        def load_w(q):
+            nc.sync.dma_start(out=w_raw[:, 2 * q:2 * q + 2, :], in_=w_v[:, 2 * q:2 * q + 2, :])
+
+        def load_y(j, c0=0, c1=N_TILE):
+            nc.sync.dma_start(out=y_raw[j][:, :, c0:c1], in_=y_v[:, :, j * N_TILE + c0:j * N_TILE + c1])
+
+        load_w(0)
+        load_y(0, 0, 256)
+        load_y(0, 256, 512)
+        load_w(1)
+        load_w(2)
+        load_y(1)
+        load_w(3)
+        load_y(2)
+        load_y(3)
+
         w_codes = keep.tile([P, M_TILES * P], U32, name="w_codes", align_bytes=64)
         w_scales = keep.tile([P, M_TILES * P], U8, name="w_scales", align_bytes=64)
+        y_codes = []
+        y_scales = []
+        for j in range(CHUNKS):
+            y_codes.append(keep.tile([P, N_TILE], U32, name="y_codes%d" % j, align_bytes=64))
+            y_scales.append(keep.tile([P, N_TILE], U8, name="y_scales%d" % j, align_bytes=64))
         w_words = w_raw[:].rearrange("p m k -> p (m k)").bitcast(F32)
 
-        def interleave_y(j, pieces):
-            grp = keep.tile([P, N_TILE, PACK], BF16, name="y_grp%d" % j, align_bytes=64)
-            y_grp[j] = grp
-            for eng, c0, c1 in pieces:
-                src = y_raw[j][:, :, c0:c1].rearrange("p t c -> p c t")
-                if eng == "v":
-                    nc.vector.tensor_copy(out=grp[:, c0:c1, :], in_=src)
-                else:
-                    nc.scalar.copy(out=grp[:, c0:c1, :], in_=src)
+        w_grp = []
+        for q in range(4):
+            w_grp.append(keep.tile([P, 2, P, 2], F32, name="w_grp%d" % q, tag="shared_grp" if q == 2 else "w_grp%d" % q, align_bytes=64))
+        w_t = {}
 
-        def interleave_y_gpsimd(j, c0=0):
-            grp = keep.tile([P, N_TILE - c0, PACK], BF16, name="y_grp%d" % j, tag="shared_grp", align_bytes=64)
-            y_grp[j] = grp
-            nc.gpsimd.tensor_scalar(
-                out=grp[:],
-                in0=y_raw[j][:, :, c0:N_TILE].rearrange("p t c -> p c t"),
-                scalar1=1.0,
-                scalar2=0.0,
-                op0=ALU.mult,
-                op1=ALU.add,
-            )
-
-        def quantize_y(j, c0=0, c1=N_TILE, grp=None):
-            if j not in y_codes:
-                y_codes[j] = keep.tile([P, N_TILE], U32, name="y_codes%d" % j, align_bytes=64)
-                y_scales[j] = keep.tile([P, N_TILE], U8, name="y_scales%d" % j, align_bytes=64)
-            if grp is None:
-                grp = y_grp[j]
-            nc.vector.quantize_mx(
-                out=y_codes[j][:, c0:c1].bitcast(FP8X4),
-                scales=y_scales[j][:, c0:c1],
-                in_=grp[:].rearrange("p c t -> p (c t)"),
-            )
-
-        def transpose_w(q, grp_half, eng):
+        def transpose_w(q):
             wt = psum.tile([P, 2, 2, P], F32, name="wt", tag="bank")
             for mm in range(2):
                 for u in range(2):
                     base = 256 * (2 * q + mm)
                     nc.tensor.transpose(wt[:, mm, u, :], w_words[:, base + u:base + 256:2], ident[:])
-            if eng == "s":
-                nc.scalar.copy(out=grp_half, in_=wt[:].rearrange("p m u r -> p m r u"))
-            else:
-                nc.vector.tensor_copy(out=grp_half, in_=wt[:].rearrange("p m u r -> p m r u"))
+            w_t[q] = wt
 
-        def quantize_w(q0, pairs, grp):
-            cols = slice(2 * P * q0, 2 * P * (q0 + pairs))
+        def copy_w(q, eng):
+            if eng == "s":
+                nc.scalar.copy(out=w_grp[q][:], in_=w_t[q][:].rearrange("p m u r -> p m r u"))
+            else:
+                nc.vector.tensor_copy(out=w_grp[q][:], in_=w_t[q][:].rearrange("p m u r -> p m r u"))
+
+        def quantize_w(q):
+            cols = slice(2 * P * q, 2 * P * (q + 1))
             nc.vector.quantize_mx(
                 out=w_codes[:, cols].bitcast(FP8X4),
                 scales=w_scales[:, cols],
-                in_=grp[:].rearrange("p m r u -> p (m r u)").bitcast(BF16),
+                in_=w_grp[q][:].rearrange("p m r u -> p (m r u)").bitcast(BF16),
             )
+
+        y0_grp = keep.tile([P, N_TILE, PACK], BF16, name="y0_grp", align_bytes=64)
+        y1_head = keep.tile([P, Y1_V, PACK], BF16, name="y1_head", align_bytes=64)
+
+        def interleave(eng, out, j, c0, c1):
+            src = y_raw[j][:, :, c0:c1].rearrange("p t c -> p c t")
+            if eng == "v":
+                nc.vector.tensor_copy(out=out, in_=src)
+            elif eng == "s":
+                nc.scalar.copy(out=out, in_=src)
+            else:
+                nc.gpsimd.tensor_scalar(out=out, in0=src, scalar1=1.0, scalar2=0.0, op0=ALU.mult, op1=ALU.add)
+
+        def quantize_y(grp, j, c0=0, c1=N_TILE):
+            nc.vector.quantize_mx(
+                out=y_codes[j][:, c0:c1].bitcast(FP8X4),
+                scales=y_scales[j][:, c0:c1],
+                in_=grp.rearrange("p c t -> p (c t)"),
+            )
+
+        y_grp = {}
+
+        def gpsimd_interleave(j, c0=0):
+            y_grp[j] = keep.tile([P, N_TILE - c0, PACK], BF16, name="y_grp%d" % j, tag="shared_grp", align_bytes=64)
+            interleave("g", y_grp[j][:], j, c0, N_TILE)
 
         stats = keep.tile([P, M_TILES, CHUNKS * 6], F32, name="stats")
         mv = keep.tile([P, M_TILES, 2], F32, name="mv")
         res = []
         for m in range(M_TILES):
             res.append(keep.tile([P, N], F32, name="res%d" % m))
-        pending = []
         sums = keep.tile([P, M_TILES], F32, name="sums")
         dev2 = keep.tile([P, M_TILES], F32, name="dev2")
         g32 = keep.tile([P, M_TILES], F32, name="g32")
@@ -151,15 +159,15 @@ def tile_nonlocalblocknd_pc_kernel(tc, y, w_w, w_b, bn_gamma, out_0, out_1, out_
         rs = keep.tile([P, M_TILES], F32, name="rs")
         gain = keep.tile([P, M_TILES], F32, name="gain")
         mean = keep.tile([P, M_TILES], F32, name="mean")
-        late = []
-        held = []
+        acc = {}
+        first_s = M_TILES - S_LAST
+        last_span = slice(N - N_TILE, N)
 
-        def bank(m, j, scalar_stats=False, hold_vector=False):
+        def multiply(m, j):
             cols = slice(P * m, P * (m + 1))
-            span = slice(j * N_TILE, (j + 1) * N_TILE)
-            acc = psum.tile([P, N_TILE], F32, name="acc", tag="bank")
+            bank = psum.tile([P, N_TILE], F32, name="acc", tag="bank")
             nc.tensor.matmul_mx(
-                out=acc[:],
+                out=bank[:],
                 lhsT=w_codes[:, cols].bitcast(FP8X4),
                 lhsT_scale=w_scales[:, cols],
                 rhs=y_codes[j][:].bitcast(FP8X4),
@@ -167,83 +175,80 @@ def tile_nonlocalblocknd_pc_kernel(tc, y, w_w, w_b, bn_gamma, out_0, out_1, out_
                 start=True,
                 stop=True,
             )
-            if scalar_stats:
-                nc.scalar.activation(out=res[m][:, span], in_=acc[:], func=ACT.Identity, bias=b_sb[:, m:m + 1], scale=1.0,
-                                     accum_out=sums[:, m:m + 1])
-                late.append((m, span))
-            else:
-                nc.scalar.activation(out=res[m][:, span], in_=acc[:], func=ACT.Identity, bias=b_sb[:, m:m + 1], scale=1.0)
-                if hold_vector:
-                    held.append(lambda: nc.vector.bn_stats(out=stats[:, m, 6 * j:6 * (j + 1)], in_=res[m][:, span]))
-                else:
-                    nc.vector.bn_stats(out=stats[:, m, 6 * j:6 * (j + 1)], in_=res[m][:, span])
-            nc.sync.dma_start(out=o_v[:, m, span], in_=res[m][:, span])
-            if not scalar_stats and not hold_vector:
-                for done_m in pending:
-                    nc.vector.bn_aggr(out=mv[:, done_m, :], in_=stats[:, done_m, :])
-                pending.clear()
-            if j == CHUNKS - 1 and not scalar_stats:
-                pending.append(m)
+            acc[m, j] = bank
 
-        nc.vector.memset(stats[:, M_TILES - S_LAST:M_TILES, 18:19], float(N_TILE))
+        def copy_out(m, j):
+            span = slice(j * N_TILE, (j + 1) * N_TILE)
+            if j == CHUNKS - 1 and m >= first_s:
+                nc.scalar.activation(out=res[m][:, span], in_=acc[m, j][:], func=ACT.Identity, bias=b_sb[:, m:m + 1], scale=1.0,
+                                     accum_out=sums[:, m:m + 1])
+            else:
+                nc.scalar.activation(out=res[m][:, span], in_=acc[m, j][:], func=ACT.Identity, bias=b_sb[:, m:m + 1], scale=1.0)
+            nc.sync.dma_start(out=o_v[:, m, span], in_=res[m][:, span])
+
+        def take_stats(m, j):
+            nc.vector.bn_stats(out=stats[:, m, 6 * j:6 * (j + 1)], in_=res[m][:, j * N_TILE:(j + 1) * N_TILE])
+
+        nc.vector.memset(stats[:, first_s:M_TILES, 18:19], float(N_TILE))
         nc.vector.memset(ones[:], 1.0)
-        nc.vector.tensor_scalar(out=stats[:, M_TILES - S_LAST:M_TILES, 20], in0=ones[:], scalar1=N * BN_EPS, scalar2=None, op0=ALU.mult)
+        nc.vector.tensor_scalar(out=stats[:, first_s:M_TILES, 20], in0=ones[:], scalar1=N * BN_EPS, scalar2=None, op0=ALU.mult)
         nc.vector.tensor_copy(out=g32[:], in_=g_sb[:])
 
-        w_grp0 = keep.tile([P, 2, P, 2], F32, name="w_grp0", align_bytes=64)
-        w_grp1 = keep.tile([P, 2, P, 2], F32, name="w_grp1", align_bytes=64)
-        w_grp23 = keep.tile([P, 4, P, 2], F32, name="w_grp23", tag="shared_grp", align_bytes=64)
-        transpose_w(0, w_grp0[:], "s")
+        transpose_w(0)
         dummies(WARM2, "warm2")
-        interleave_y(0, Y0_PIECES)
-        quantize_w(0, 1, w_grp0)
-        quantize_y(0)
-        transpose_w(1, w_grp1[:], "s")
-        transpose_w(2, w_grp23[:, 0:2, :, :], "s")
-        transpose_w(3, w_grp23[:, 2:4, :, :], "s")
-        quantize_w(1, 1, w_grp1)
-        y1_head = keep.tile([P, Y1_V, PACK], BF16, name="y1_head", align_bytes=64)
-        nc.vector.tensor_copy(out=y1_head[:], in_=y_raw[1][:, :, 0:Y1_V].rearrange("p t c -> p c t"))
-        quantize_w(2, 2, w_grp23)
-        interleave_y_gpsimd(1, Y1_V)
-        quantize_y(1, 0, Y1_V, y1_head)
+        copy_w(0, "s")
+        interleave("v", y0_grp[:, 0:256, :], 0, 0, 256)
+        interleave("v", y0_grp[:, 256:Y0_S, :], 0, 256, Y0_S)
+        quantize_w(0)
+        quantize_y(y0_grp[:], 0)
+        transpose_w(1)
+        transpose_w(2)
+        copy_w(1, "s")
+        copy_w(2, W2_E)
+        quantize_w(1)
+        interleave("v", y1_head[:], 1, 0, Y1_V)
+        quantize_w(2)
+        gpsimd_interleave(1, Y1_V)
+        quantize_y(y1_head[:], 1, 0, Y1_V)
         order = [(m, j) for j in range(CHUNKS) for m in range(M_TILES)]
         for i in range(len(order)):
-            bank(order[i][0], order[i][1], i >= len(order) - S_LAST, i == len(order) - S_LAST - 1)
-            for c in range(1, CHUNKS):
-                if i == QUANT_AT[c]:
-                    if c == 1:
-                        quantize_y(c, Y1_V, N_TILE)
-                    else:
-                        quantize_y(c)
-                    if c + 1 < CHUNKS:
-                        interleave_y_gpsimd(c + 1)
-        first_s = M_TILES - S_LAST
-        first_c = M_TILES - S_COLS
-        for m, span in late:
+            m, j = order[i]
+            multiply(m, j)
+            copy_out(m, j)
+            if i == 1:
+                transpose_w(3)
+            if i == 1:
+                copy_w(3, W3_E)
+            if j < CHUNKS - 1 or m < first_s:
+                take_stats(m, j)
+            if j == CHUNKS - 1 and 0 < m < first_s:
+                nc.vector.bn_aggr(out=mv[:, m - 1, :], in_=stats[:, m - 1, :])
+            if i == 2:
+                quantize_w(3)
+            if i == 2:
+                quantize_y(y_grp[1][:], 1, Y1_V, N_TILE)
+                gpsimd_interleave(2)
+            if i == 8:
+                quantize_y(y_grp[2][:], 2)
+                gpsimd_interleave(3)
+            if i == 15:
+                quantize_y(y_grp[3][:], 3)
+
+        for m in range(first_s, M_TILES):
             nc.scalar.mul(out=stats[:, m, 19:20], in_=sums[:, m:m + 1], mul=1.0 / N_TILE)
-        for m, span in late:
+        for m in range(first_s, M_TILES):
             nc.vector.bn_aggr(out=mv[:, m, :], in_=stats[:, m, 0:21])
-        for v_step in held:
-            v_step()
-        for done_m in pending:
-            nc.vector.bn_aggr(out=mv[:, done_m, :], in_=stats[:, done_m, :])
-        for m, span in late:
+        nc.vector.bn_aggr(out=mv[:, first_s - 1, :], in_=stats[:, first_s - 1, :])
+        for m in range(first_s, M_TILES):
             scrap = keep.tile([P, N_TILE], F32, name="scrap%d" % m)
-            nc.scalar.activation(out=scrap[:], in_=res[m][:, span], func=ACT.Square, bias=stats[:, m, 19:20], scale=-1.0,
+            nc.scalar.activation(out=scrap[:], in_=res[m][:, last_span], func=ACT.Square, bias=stats[:, m, 19:20], scale=-1.0,
                                  accum_out=dev2[:, m:m + 1])
-            if m == first_s:
-                nc.scalar.activation(out=rs[:, 0:first_c], in_=mv[:, 0:first_c, 1], func=ACT.Abs_reciprocal_sqrt, bias=BN_EPS, scale=1.0)
-        for m, span in late:
+        nc.scalar.activation(out=rs[:, 0:first_s], in_=mv[:, 0:first_s, 1], func=ACT.Abs_reciprocal_sqrt, bias=BN_EPS, scale=1.0)
+        for m in range(first_s, M_TILES):
             nc.scalar.activation(out=rs[:, m:m + 1], in_=dev2[:, m:m + 1], func=ACT.Abs_reciprocal_sqrt, bias=mv[:, m, 1:2], scale=1.0 / N)
-        for m in range(first_c, first_s - 1):
-            nc.scalar.activation(out=rs[:, m:m + 1], in_=mv[:, m, 1:2], func=ACT.Abs_reciprocal_sqrt, bias=BN_EPS, scale=1.0)
-        for m in list(range(first_s, M_TILES)) + list(range(first_c, first_s - 1)):
+        for m in range(first_s, M_TILES):
             nc.scalar.activation(out=gain[:, m:m + 1], in_=rs[:, m:m + 1], func=ACT.Copy, scale=g32[:, m:m + 1])
-        m = first_s - 1
-        nc.scalar.activation(out=rs[:, m:m + 1], in_=mv[:, m, 1:2], func=ACT.Abs_reciprocal_sqrt, bias=BN_EPS, scale=1.0)
-        nc.scalar.activation(out=gain[:, m:m + 1], in_=rs[:, m:m + 1], func=ACT.Copy, scale=g32[:, m:m + 1])
-        nc.vector.tensor_mul(out=gain[:, 0:first_c], in0=rs[:, 0:first_c], in1=g_sb[:, 0:first_c])
+        nc.vector.tensor_mul(out=gain[:, 0:first_s], in0=rs[:, 0:first_s], in1=g_sb[:, 0:first_s])
         nc.scalar.dma_start(out=out_2.rearrange("(p m) -> p m", m=M_TILES), in_=gain[:])
         nc.vector.tensor_copy(out=mean[:], in_=mv[:, :, 0])
         nc.sync.dma_start(out=out_1.rearrange("(p m) -> p m", m=M_TILES), in_=mean[:])

@@ -26,7 +26,7 @@ BN_EPS = 1e-5
 WARM = 4
 WARM2 = 3
 S_LAST = 2
-Y0_S = 512
+Y0_S = 384
 Y1_V = 256
 W3_E = "s"
 W2_E = "s"
@@ -199,8 +199,10 @@ def tile_nonlocalblocknd_pc_kernel(tc, y, w_w, w_b, bn_gamma, out_0, out_1, out_
         copy_w(0, "s")
         interleave("v", y0_grp[:, 0:256, :], 0, 0, 256)
         interleave("v", y0_grp[:, 256:Y0_S, :], 0, 256, Y0_S)
+        interleave("s", y0_grp[:, Y0_S:N_TILE, :], 0, Y0_S, N_TILE)
         quantize_w(0)
-        quantize_y(y0_grp[:], 0)
+        quantize_y(y0_grp[:, 0:256, :], 0, 0, 256)
+        quantize_y(y0_grp[:, 256:N_TILE, :], 0, 256, N_TILE)
         transpose_w(1)
         transpose_w(2)
         copy_w(1, "s")

from contextlib import ExitStack

import concourse.mybir as mybir
from concourse.masks import make_identity

FLOPS = 2 * 1024 * 512 * 2048

F32 = mybir.dt.float32
BF16 = mybir.dt.bfloat16
U32 = mybir.dt.uint32
U8 = mybir.dt.uint8
FP8X4 = mybir.dt.float8_e5m2_x4
ACT = mybir.ActivationFunctionType
ALU = mybir.AluOpType

P = 128
C_OUT = 1024
K = 512
N = 2048
PACK = 4
M_TILES = C_OUT // P
N_TILE = 512
CHUNKS = N // N_TILE
BN_EPS = 1e-5

WARM = 4
WARM2 = 3
S_LAST = 2
Y0_S = 384
Y1_V = 256
W3_E = "s"
W2_E = "s"


def tile_nonlocalblocknd_pc_kernel(tc, y, w_w, w_b, bn_gamma, out_0, out_1, out_2):
    nc = tc.nc
    y_v = y.rearrange("b d t h w -> (b d) (t h w)").rearrange("(p j) n -> p j n", j=PACK)
    w_v = w_w.rearrange("(p m) k -> p m k", m=M_TILES)
    o_v = out_0.rearrange("b c t h w -> (b c) (t h w)").rearrange("(p m) n -> p m n", m=M_TILES)

    with ExitStack() as ctx:
        ctx.enter_context(tc.manual_schedule())
        keep = ctx.enter_context(tc.tile_pool(name="keep", bufs=1))
        psum = ctx.enter_context(tc.psum_pool(name="psum", bufs=8))

        b_sb = keep.tile([P, M_TILES], BF16, name="b_sb")
        g_sb = keep.tile([P, M_TILES], BF16, name="g_sb")
        nc.scalar.dma_start(out=b_sb[:], in_=w_b.rearrange("(p m) -> p m", m=M_TILES))
        nc.scalar.dma_start(out=g_sb[:], in_=bn_gamma.rearrange("(p m) -> p m", m=M_TILES))

        zeros = keep.tile([P, N_TILE], BF16, name="zeros")
        nc.vector.memset(zeros[:], 0.0)
        one = keep.tile([P, 1], F32, name="one")
        junk = keep.tile([P, 1], F32, name="junk")
        nc.vector.memset(one[:], 1.0)
        nc.scalar.activation(out=junk[:], in_=one[:], func=ACT.Abs_reciprocal_sqrt)

        ident = keep.tile([P, P], F32, name="ident")
        make_identity(nc, ident[:])

        def dummies(count, name):
            warm = psum.tile([P, N_TILE], F32, name=name, tag="bank")
            for i in range(count):
                nc.tensor.matmul(warm[:], lhsT=zeros[:, 0:P], rhs=zeros[:], start=True, stop=True)

        dummies(WARM, "warm")

        w_raw = keep.tile([P, M_TILES, K], BF16, name="w_raw")
        y_raw = []
        for j in range(CHUNKS):
            y_raw.append(keep.tile([P, PACK, N_TILE], BF16, name="y_raw%d" % j))

        def load_w(q):
            nc.sync.dma_start(out=w_raw[:, 2 * q:2 * q + 2, :], in_=w_v[:, 2 * q:2 * q + 2, :])

        def load_y(j, c0=0, c1=N_TILE):
            nc.sync.dma_start(out=y_raw[j][:, :, c0:c1], in_=y_v[:, :, j * N_TILE + c0:j * N_TILE + c1])

        load_w(0)
        load_y(0, 0, 256)
        load_y(0, 256, 512)
        load_w(1)
        load_w(2)
        load_y(1)
        load_w(3)
        load_y(2)
        load_y(3)

        w_codes = keep.tile([P, M_TILES * P], U32, name="w_codes", align_bytes=64)
        w_scales = keep.tile([P, M_TILES * P], U8, name="w_scales", align_bytes=64)
        y_codes = []
        y_scales = []
        for j in range(CHUNKS):
            y_codes.append(keep.tile([P, N_TILE], U32, name="y_codes%d" % j, align_bytes=64))
            y_scales.append(keep.tile([P, N_TILE], U8, name="y_scales%d" % j, align_bytes=64))
        w_words = w_raw[:].rearrange("p m k -> p (m k)").bitcast(F32)

        w_grp = []
        for q in range(4):
            w_grp.append(keep.tile([P, 2, P, 2], F32, name="w_grp%d" % q, tag="shared_grp" if q == 2 else "w_grp%d" % q, align_bytes=64))
        w_t = {}

        def transpose_w(q):
            wt = psum.tile([P, 2, 2, P], F32, name="wt", tag="bank")
            for mm in range(2):
                for u in range(2):
                    base = 256 * (2 * q + mm)
                    nc.tensor.transpose(wt[:, mm, u, :], w_words[:, base + u:base + 256:2], ident[:])
            w_t[q] = wt

        def copy_w(q, eng):
            if eng == "s":
                nc.scalar.copy(out=w_grp[q][:], in_=w_t[q][:].rearrange("p m u r -> p m r u"))
            else:
                nc.vector.tensor_copy(out=w_grp[q][:], in_=w_t[q][:].rearrange("p m u r -> p m r u"))

        def quantize_w(q):
            cols = slice(2 * P * q, 2 * P * (q + 1))
            nc.vector.quantize_mx(
                out=w_codes[:, cols].bitcast(FP8X4),
                scales=w_scales[:, cols],
                in_=w_grp[q][:].rearrange("p m r u -> p (m r u)").bitcast(BF16),
            )

        y0_grp = keep.tile([P, N_TILE, PACK], BF16, name="y0_grp", align_bytes=64)
        y1_head = keep.tile([P, Y1_V, PACK], BF16, name="y1_head", align_bytes=64)

        def interleave(eng, out, j, c0, c1):
            src = y_raw[j][:, :, c0:c1].rearrange("p t c -> p c t")
            if eng == "v":
                nc.vector.tensor_copy(out=out, in_=src)
            elif eng == "s":
                nc.scalar.copy(out=out, in_=src)
            else:
                nc.gpsimd.tensor_scalar(out=out, in0=src, scalar1=1.0, scalar2=0.0, op0=ALU.mult, op1=ALU.add)

        def quantize_y(grp, j, c0=0, c1=N_TILE):
            nc.vector.quantize_mx(
                out=y_codes[j][:, c0:c1].bitcast(FP8X4),
                scales=y_scales[j][:, c0:c1],
                in_=grp.rearrange("p c t -> p (c t)"),
            )

        y_grp = {}

        def gpsimd_interleave(j, c0=0):
            y_grp[j] = keep.tile([P, N_TILE - c0, PACK], BF16, name="y_grp%d" % j, tag="shared_grp", align_bytes=64)
            interleave("g", y_grp[j][:], j, c0, N_TILE)

        stats = keep.tile([P, M_TILES, CHUNKS * 6], F32, name="stats")
        mv = keep.tile([P, M_TILES, 2], F32, name="mv")
        res = []
        for m in range(M_TILES):
            res.append(keep.tile([P, N], F32, name="res%d" % m))
        sums = keep.tile([P, M_TILES], F32, name="sums")
        dev2 = keep.tile([P, M_TILES], F32, name="dev2")
        g32 = keep.tile([P, M_TILES], F32, name="g32")
        ones = keep.tile([P, S_LAST], F32, name="ones")
        rs = keep.tile([P, M_TILES], F32, name="rs")
        gain = keep.tile([P, M_TILES], F32, name="gain")
        mean = keep.tile([P, M_TILES], F32, name="mean")
        acc = {}
        first_s = M_TILES - S_LAST
        last_span = slice(N - N_TILE, N)

        def multiply(m, j):
            cols = slice(P * m, P * (m + 1))
            bank = psum.tile([P, N_TILE], F32, name="acc", tag="bank")
            nc.tensor.matmul_mx(
                out=bank[:],
                lhsT=w_codes[:, cols].bitcast(FP8X4),
                lhsT_scale=w_scales[:, cols],
                rhs=y_codes[j][:].bitcast(FP8X4),
                rhs_scale=y_scales[j][:],
                start=True,
                stop=True,
            )
            acc[m, j] = bank

        def copy_out(m, j):
            span = slice(j * N_TILE, (j + 1) * N_TILE)
            if j == CHUNKS - 1 and m >= first_s:
                nc.scalar.activation(out=res[m][:, span], in_=acc[m, j][:], func=ACT.Identity, bias=b_sb[:, m:m + 1], scale=1.0,
                                     accum_out=sums[:, m:m + 1])
            else:
                nc.scalar.activation(out=res[m][:, span], in_=acc[m, j][:], func=ACT.Identity, bias=b_sb[:, m:m + 1], scale=1.0)
            nc.sync.dma_start(out=o_v[:, m, span], in_=res[m][:, span])

        def take_stats(m, j):
            nc.vector.bn_stats(out=stats[:, m, 6 * j:6 * (j + 1)], in_=res[m][:, j * N_TILE:(j + 1) * N_TILE])

        nc.vector.memset(stats[:, first_s:M_TILES, 18:19], float(N_TILE))
        nc.vector.memset(ones[:], 1.0)
        nc.vector.tensor_scalar(out=stats[:, first_s:M_TILES, 20], in0=ones[:], scalar1=N * BN_EPS, scalar2=None, op0=ALU.mult)
        nc.vector.tensor_copy(out=g32[:], in_=g_sb[:])

        transpose_w(0)
        dummies(WARM2, "warm2")
        copy_w(0, "s")
        interleave("v", y0_grp[:, 0:256, :], 0, 0, 256)
        interleave("v", y0_grp[:, 256:Y0_S, :], 0, 256, Y0_S)
        interleave("s", y0_grp[:, Y0_S:N_TILE, :], 0, Y0_S, N_TILE)
        quantize_w(0)
        quantize_y(y0_grp[:, 0:256, :], 0, 0, 256)
        quantize_y(y0_grp[:, 256:N_TILE, :], 0, 256, N_TILE)
        transpose_w(1)
        transpose_w(2)
        copy_w(1, "s")
        copy_w(2, W2_E)
        quantize_w(1)
        interleave("v", y1_head[:], 1, 0, Y1_V)
        quantize_w(2)
        gpsimd_interleave(1, Y1_V)
        quantize_y(y1_head[:], 1, 0, Y1_V)
        order = [(m, j) for j in range(CHUNKS) for m in range(M_TILES)]
        for i in range(len(order)):
            m, j = order[i]
            multiply(m, j)
            copy_out(m, j)
            if i == 1:
                transpose_w(3)
            if i == 1:
                copy_w(3, W3_E)
            if j < CHUNKS - 1 or m < first_s:
                take_stats(m, j)
            if j == CHUNKS - 1 and 0 < m < first_s:
                nc.vector.bn_aggr(out=mv[:, m - 1, :], in_=stats[:, m - 1, :])
            if i == 2:
                quantize_w(3)
            if i == 2:
                quantize_y(y_grp[1][:], 1, Y1_V, N_TILE)
                gpsimd_interleave(2)
            if i == 8:
                quantize_y(y_grp[2][:], 2)
                gpsimd_interleave(3)
            if i == 15:
                quantize_y(y_grp[3][:], 3)

        for m in range(first_s, M_TILES):
            nc.scalar.mul(out=stats[:, m, 19:20], in_=sums[:, m:m + 1], mul=1.0 / N_TILE)
        for m in range(first_s, M_TILES):
            nc.vector.bn_aggr(out=mv[:, m, :], in_=stats[:, m, 0:21])
        nc.vector.bn_aggr(out=mv[:, first_s - 1, :], in_=stats[:, first_s - 1, :])
        for m in range(first_s, M_TILES):
            scrap = keep.tile([P, N_TILE], F32, name="scrap%d" % m)
            nc.scalar.activation(out=scrap[:], in_=res[m][:, last_span], func=ACT.Square, bias=stats[:, m, 19:20], scale=-1.0,
                                 accum_out=dev2[:, m:m + 1])
        nc.scalar.activation(out=rs[:, 0:first_s], in_=mv[:, 0:first_s, 1], func=ACT.Abs_reciprocal_sqrt, bias=BN_EPS, scale=1.0)
        for m in range(first_s, M_TILES):
            nc.scalar.activation(out=rs[:, m:m + 1], in_=dev2[:, m:m + 1], func=ACT.Abs_reciprocal_sqrt, bias=mv[:, m, 1:2], scale=1.0 / N)
        for m in range(first_s, M_TILES):
            nc.scalar.activation(out=gain[:, m:m + 1], in_=rs[:, m:m + 1], func=ACT.Copy, scale=g32[:, m:m + 1])
        nc.vector.tensor_mul(out=gain[:, 0:first_s], in0=rs[:, 0:first_s], in1=g_sb[:, 0:first_s])
        nc.scalar.dma_start(out=out_2.rearrange("(p m) -> p m", m=M_TILES), in_=gain[:])
        nc.vector.tensor_copy(out=mean[:], in_=mv[:, :, 0])
        nc.sync.dma_start(out=out_1.rearrange("(p m) -> p m", m=M_TILES), in_=mean[:])
